import numpy as np
import ml_dtypes


def mxq(x, axis, fmt="e4m3"):
    dtype, down = {"e4m3": (ml_dtypes.float8_e4m3fn, 7), "e5m2": (ml_dtypes.float8_e5m2, 14)}[fmt]
    v = np.moveaxis(np.asarray(x, np.float32).astype(ml_dtypes.bfloat16).astype(np.float64), axis, -1)
    blocks = v.reshape(v.shape[:-1] + (-1, 32))
    amax = np.abs(blocks).max(-1, keepdims=True)
    byte = np.maximum(np.where(amax > 0, np.frexp(amax)[1] - 1 + 127, 0) - down, 1)
    scale = np.exp2(byte - 127.0)
    codes = (blocks / scale).astype(np.float32).astype(dtype).astype(np.float64)
    return np.moveaxis((codes * scale).reshape(v.shape), -1, axis)


WIDE = False


def mx_kscale(k):
    if not WIDE:
        return np.ones(k)
    levels = np.array([10, -10, 5, -5, 0])
    a = np.random.permutation(np.resize(levels, k // 512 * 4)).reshape(k // 512, 4)
    idx = np.arange(k)
    return np.exp2(a[idx // 512, idx % 128 // 32])


BF16 = ml_dtypes.bfloat16


def bf(x):
    return np.asarray(x, np.float32).astype(BF16)


def f64(x):
    return np.asarray(x).astype(np.float64)


N, NS, NV, H, XYZ = 4096, 512, 512, 4, 3
D = NS // H
COMB = NS + NV
EPS_NORM = 1e-8


def norm_no_nan(x):
    return np.sqrt(np.maximum(np.sum(np.square(x), axis=-1), EPS_NORM))


def setup_inputs():
    c = mx_kscale(COMB)
    cs, cv = c[:NS], c[NS:]
    return {"s": bf(np.random.standard_normal((N, NS)) * cs),
            "v": bf(np.random.standard_normal((N, NV, XYZ)) * 0.6 * cv[:, None]),
            "Wq": bf(np.random.standard_normal((COMB, NS)) * 1.6 / np.sqrt(COMB) / c[:, None]),
            "bq": bf(np.random.standard_normal(NS) * 0.2),
            "Wk": bf(np.random.standard_normal((COMB, NS)) * 1.6 / np.sqrt(COMB) / c[:, None]),
            "bk": bf(np.random.standard_normal(NS) * 0.2)}


def reference(s, v, Wq, bq, Wk, bk):
    v_norm = norm_no_nan(f64(v))
    comb = np.concatenate([f64(s), v_norm], axis=-1)
    cq = mxq(comb, 1, "e4m3")
    q = ((cq @ mxq(f64(Wq), 0, "e4m3")) + f64(bq)).reshape(N, H, D)
    k = ((cq @ mxq(f64(Wk), 0, "e4m3")) + f64(bk)).reshape(N, H, D)
    return q, k

@@ -1,0 +1,231 @@
+from contextlib import ExitStack
+
+import concourse.mybir as mybir
+from concourse.masks import make_identity
+
+F32 = mybir.dt.float32
+BF16 = mybir.dt.bfloat16
+U32 = mybir.dt.uint32
+U8 = mybir.dt.uint8
+FP8X4 = mybir.dt.float8_e4m3fn_x4
+ACT = mybir.ActivationFunctionType
+ALU = mybir.AluOpType
+
+P = 128
+PACK = 4
+NODES = 4096
+NS = 512
+NV = 512
+XYZ = 3
+OUT = 512
+PASSES = 2
+TILES = NODES // P
+ROUND = 2
+ROUNDS = TILES // ROUND
+AHEAD = 10
+NORM_FLOOR = 1e-4
+SQRT_GUARD = 2.0 ** -100
+
+FLOPS = 2 * NODES * (NS + NV) * (2 * OUT)
+
+
+def tile_multiattentivegvplayer_pa_t_kernel(tc, s, v, Wq, bq, Wk, bk, out_0, out_1):
+    nc = tc.nc
+    weights = (Wq, Wk)
+    biases = (bq, bk)
+
+    s_view = s.rearrange("(p t) k -> p t k", t=TILES)
+    v_view = v.rearrange("(p t) j c -> p t (j c)", t=TILES)
+    out_views = (
+        out_0.rearrange("(p t) h d -> p t (h d)", t=TILES),
+        out_1.rearrange("(p t) h d -> p t (h d)", t=TILES),
+    )
+
+    with ExitStack() as ctx:
+        ctx.enter_context(tc.manual_schedule())
+        const = ctx.enter_context(tc.tile_pool(name="const", bufs=1))
+        loads = ctx.enter_context(tc.tile_pool(name="loads", bufs=AHEAD))
+        squares = ctx.enter_context(tc.tile_pool(name="squares", bufs=2 * ROUND))
+        operands = ctx.enter_context(tc.tile_pool(name="operands", bufs=2))
+        results = ctx.enter_context(tc.tile_pool(name="results", bufs=3))
+        psum = ctx.enter_context(tc.psum_pool(name="psum", bufs=1))
+
+        s_tiles = {}
+        v_tiles = {}
+        sq_tiles = {}
+        sumsq_tiles = {}
+        grouped_tiles = {}
+        code_tiles = {}
+
+        def load_round(r):
+            tiles_of_round = slice(r * ROUND, (r + 1) * ROUND)
+            v_sb = loads.tile([P, ROUND, NV * XYZ], BF16, name="v_sb")
+            nc.sync.dma_start(out=v_sb[:], in_=v_view[:, tiles_of_round, :])
+            s_sb = loads.tile([P, ROUND, NS], BF16, name="s_sb")
+            nc.sync.dma_start(out=s_sb[:], in_=s_view[:, tiles_of_round, :])
+            v_tiles[r] = v_sb
+            s_tiles[r] = s_sb
+
+        def square_round(r):
+            sq_tiles[r] = []
+            for i in range(ROUND):
+                sq = squares.tile([P, XYZ, NV], F32, name="sq")
+                nc.scalar.activation(
+                    out=sq[:],
+                    in_=v_tiles[r][:, i, :].rearrange("p (j c) -> p c j", c=XYZ),
+                    func=ACT.Square,
+                )
+                sq_tiles[r].append(sq)
+
+        def transpose_round(r):
+            s_words = s_tiles[r][:].bitcast(F32)
+            s_t = psum.tile([P, ROUND, 2, P], F32, name="s_t")
+            for i in range(ROUND):
+                for u in range(2):
+                    nc.tensor.transpose(
+                        out=s_t[:, i, u, :],
+                        in_=s_words[:, i, u * P : (u + 1) * P],
+                        identity=ident[:],
+                    )
+            sumsq_tiles[r] = []
+            for i in range(ROUND):
+                sumsq = psum.tile([P, PACK, P], F32, name="sumsq", bufs=3)
+                for t in range(PACK):
+                    for c in range(XYZ):
+                        nc.tensor.matmul(
+                            out=sumsq[:, t, :],
+                            lhsT=sq_tiles[r][i][:, c, t * P : (t + 1) * P],
+                            rhs=ident[:],
+                            is_transpose=True,
+                            start=(c == 0),
+                            stop=(c == XYZ - 1),
+                        )
+                sumsq_tiles[r].append(sumsq)
+            return s_t
+
+        def copy_s_round(r, s_t):
+            grouped = operands.tile([P, PASSES, ROUND, P, PACK], BF16, name="grouped", align_bytes=64)
+            nc.vector.tensor_copy(
+                out=grouped[:, 0].bitcast(F32),
+                in_=s_t[:].rearrange("p i u n -> p i n u"),
+            )
+            grouped_tiles[r] = grouped
+
+        def root_round(r):
+            for i in range(ROUND):
+                nc.scalar.activation(
+                    out=grouped_tiles[r][:, 1, i],
+                    in_=sumsq_tiles[r][i][:].rearrange("p t n -> p n t"),
+                    func=ACT.Sqrt,
+                    bias=guard[:],
+                )
+
+        def floor_round(r):
+            norms = grouped_tiles[r][:, 1]
+            nc.vector.tensor_scalar_max(out=norms, in0=norms, scalar1=NORM_FLOOR)
+
+        def quantise_round(r):
+            codes = operands.tile([P, PASSES, ROUND, P], U32, name="codes", align_bytes=64)
+            scales = operands.tile([P, PASSES, ROUND, P], U8, name="scales", align_bytes=64)
+            nc.vector.quantize_mx(
+                out=codes[:].rearrange("p c i n -> p (c i n)").bitcast(FP8X4),
+                scales=scales[:].rearrange("p c i n -> p (c i n)"),
+                in_=grouped_tiles[r][:].rearrange("p c i n t -> p (c i n t)"),
+            )
+            code_tiles[r] = (codes, scales)
+
+        def project_round(r):
+            codes, scales = code_tiles[r]
+            tiles_of_round = slice(r * ROUND, (r + 1) * ROUND)
+            out_sb = [
+                results.tile([P, ROUND, OUT], F32, name="q_sb"),
+                results.tile([P, ROUND, OUT], F32, name="k_sb"),
+            ]
+            for i in range(ROUND):
+                for m in range(2):
+                    acc = psum.tile([P, OUT], F32, name="acc", bufs=4)
+                    for c in range(PASSES):
+                        nc.tensor.matmul_mx(
+                            out=acc[:],
+                            lhsT=codes[:, c, i, :].bitcast(FP8X4),
+                            lhsT_scale=scales[:, c, i, :],
+                            rhs=w_codes[:, m, c, :].bitcast(FP8X4),
+                            rhs_scale=w_scales[:, m, c, :],
+                            start=(c == 0),
+                            stop=(c == PASSES - 1),
+                        )
+                    nc.vector.tensor_tensor(
+                        out=out_sb[m][:, i, :], in0=acc[:], in1=bias[:, m, :], op=ALU.add
+                    )
+            for m in range(2):
+                nc.gpsimd.dma_start(out=out_views[m][:, tiles_of_round, :], in_=out_sb[m][:])
+
+        guard = const.tile([P, 1], F32, name="guard")
+        nc.vector.memset(guard[:], SQRT_GUARD)
+        warm = const.tile([P, 1], F32, name="warm")
+        nc.scalar.activation(out=warm[:], in_=guard[:], func=ACT.Sqrt)
+        ident = const.tile([P, P], F32, name="ident")
+        make_identity(nc, ident[:])
+        ones = const.tile([P, P], BF16, name="ones")
+        nc.vector.memset(ones[:], 1.0)
+        bias_rows = const.tile([P, 2, OUT], BF16, name="bias_rows")
+        nc.vector.memset(bias_rows[:], 0.0)
+
+        load_round(0)
+        for m in range(2):
+            nc.sync.dma_start(
+                out=bias_rows[0:1, m, :], in_=biases[m].rearrange("(o n) -> o n", o=1)
+            )
+        load_round(1)
+        w_raw = const.tile([P, 2, PASSES, PACK, OUT], BF16, name="w_raw")
+        for m in range(2):
+            nc.sync.dma_start(
+                out=w_raw[:, m, 0].rearrange("p (u e) n -> p u e n", e=2),
+                in_=weights[m][0:NS, :].rearrange("(u p e) n -> p u e n", u=2, e=2),
+            )
+            nc.sync.dma_start(
+                out=w_raw[:, m, 1],
+                in_=weights[m][NS : NS + NV, :].rearrange("(t p) n -> p t n", p=P),
+            )
+        for r in range(2, AHEAD):
+            load_round(r)
+
+        bias = const.tile([P, 2, OUT], F32, name="bias")
+        for m in range(2):
+            acc = psum.tile([P, OUT], F32, name="acc", bufs=4)
+            nc.tensor.matmul(out=acc[:], lhsT=ones[:], rhs=bias_rows[:, m, :], start=True, stop=True)
+            nc.vector.tensor_copy(out=bias[:, m, :], in_=acc[:])
+
+        w_grouped = const.tile([P, 2, PASSES, OUT, PACK], BF16, name="w_grouped", align_bytes=64)
+        w_codes = const.tile([P, 2, PASSES, OUT], U32, name="w_codes", align_bytes=64)
+        w_scales = const.tile([P, 2, PASSES, OUT], U8, name="w_scales", align_bytes=64)
+        for m in range(2):
+            for c in range(PASSES):
+                nc.vector.tensor_copy(
+                    out=w_grouped[:, m, c], in_=w_raw[:, m, c].rearrange("p t n -> p n t")
+                )
+        for m in range(2):
+            nc.vector.quantize_mx(
+                out=w_codes[:, m].rearrange("p c n -> p (c n)").bitcast(FP8X4),
+                scales=w_scales[:, m].rearrange("p c n -> p (c n)"),
+                in_=w_grouped[:, m].rearrange("p c n t -> p (c n t)"),
+            )
+
+        square_round(0)
+        for r in range(ROUNDS + 1):
+            if r < ROUNDS:
+                s_t = transpose_round(r)
+            if r + AHEAD < ROUNDS:
+                load_round(r + AHEAD)
+            if r >= 1:
+                floor_round(r - 1)
+            if r < ROUNDS:
+                copy_s_round(r, s_t)
+            if r >= 1:
+                quantise_round(r - 1)
+            if r + 1 < ROUNDS:
+                square_round(r + 1)
+            if r >= 1:
+                project_round(r - 1)
+            if r < ROUNDS:
+                root_round(r)

@@ -158,7 +158,7 @@ def tile_multiattentivegvplayer_pa_t_kernel(tc, s, v, Wq, bq, Wk, bk, out_0, out
                         out=out_sb[m][:, i, :], in0=acc[:], in1=bias[:, m, :], op=ALU.add
                     )
             for m in range(2):
-                nc.gpsimd.dma_start(out=out_views[m][:, tiles_of_round, :], in_=out_sb[m][:])
+                nc.sync.dma_start(out=out_views[m][:, tiles_of_round, :], in_=out_sb[m][:])
 
         guard = const.tile([P, 1], F32, name="guard")
         nc.vector.memset(guard[:], SQRT_GUARD)

@@ -75,6 +75,7 @@ def tile_multiattentivegvplayer_pa_t_kernel(tc, s, v, Wq, bq, Wk, bk, out_0, out
                     in_=v_tiles[r][:, i, :].rearrange("p (j c) -> p c j", c=XYZ),
                     func=ACT.Square,
                 )
+                nc.gpsimd.tensor_tensor(out=sq[:, 0, :], in0=sq[:, 0, :], in1=sq[:, 1, :], op=ALU.add)
                 sq_tiles[r].append(sq)
 
         def transpose_round(r):
@@ -91,7 +92,7 @@ def tile_multiattentivegvplayer_pa_t_kernel(tc, s, v, Wq, bq, Wk, bk, out_0, out
             for i in range(ROUND):
                 sumsq = psum.tile([P, PACK, P], F32, name="sumsq", bufs=3)
                 for t in range(PACK):
-                    for c in range(XYZ):
+                    for c in (0, XYZ - 1):
                         nc.tensor.matmul(
                             out=sumsq[:, t, :],
                             lhsT=sq_tiles[r][i][:, c, t * P : (t + 1) * P],

@@ -75,7 +75,6 @@ def tile_multiattentivegvplayer_pa_t_kernel(tc, s, v, Wq, bq, Wk, bk, out_0, out
                     in_=v_tiles[r][:, i, :].rearrange("p (j c) -> p c j", c=XYZ),
                     func=ACT.Square,
                 )
-                nc.gpsimd.tensor_tensor(out=sq[:, 0, :], in0=sq[:, 0, :], in1=sq[:, 1, :], op=ALU.add)
                 sq_tiles[r].append(sq)
 
         def transpose_round(r):
@@ -92,7 +91,7 @@ def tile_multiattentivegvplayer_pa_t_kernel(tc, s, v, Wq, bq, Wk, bk, out_0, out
             for i in range(ROUND):
                 sumsq = psum.tile([P, PACK, P], F32, name="sumsq", bufs=3)
                 for t in range(PACK):
-                    for c in (0, XYZ - 1):
+                    for c in range(XYZ):
                         nc.tensor.matmul(
                             out=sumsq[:, t, :],
                             lhsT=sq_tiles[r][i][:, c, t * P : (t + 1) * P],
@@ -126,8 +125,8 @@ def tile_multiattentivegvplayer_pa_t_kernel(tc, s, v, Wq, bq, Wk, bk, out_0, out
             nc.vector.tensor_scalar_max(out=norms, in0=norms, scalar1=NORM_FLOOR)
 
         def quantise_round(r):
-            codes = operands.tile([P, PASSES, ROUND, P], U32, name="codes", align_bytes=64)
-            scales = operands.tile([P, PASSES, ROUND, P], U8, name="scales", align_bytes=64)
+            codes = operands.tile([P, PASSES, ROUND, P], U32, name="codes", bufs=3, align_bytes=64)
+            scales = operands.tile([P, PASSES, ROUND, P], U8, name="scales", bufs=3, align_bytes=64)
             nc.vector.quantize_mx(
                 out=codes[:].rearrange("p c i n -> p (c i n)").bitcast(FP8X4),
                 scales=scales[:].rearrange("p c i n -> p (c i n)"),
@@ -213,20 +212,20 @@ def tile_multiattentivegvplayer_pa_t_kernel(tc, s, v, Wq, bq, Wk, bk, out_0, out
             )
 
         square_round(0)
-        for r in range(ROUNDS + 1):
+        for r in range(ROUNDS + 2):
             if r < ROUNDS:
                 s_t = transpose_round(r)
             if r + AHEAD < ROUNDS:
                 load_round(r + AHEAD)
-            if r >= 1:
+            if 1 <= r <= ROUNDS:
                 floor_round(r - 1)
             if r < ROUNDS:
                 copy_s_round(r, s_t)
-            if r >= 1:
+            if 1 <= r <= ROUNDS:
                 quantise_round(r - 1)
             if r + 1 < ROUNDS:
                 square_round(r + 1)
-            if r >= 1:
-                project_round(r - 1)
+            if r >= 2:
+                project_round(r - 2)
             if r < ROUNDS:
                 root_round(r)

@@ -75,6 +75,7 @@ def tile_multiattentivegvplayer_pa_t_kernel(tc, s, v, Wq, bq, Wk, bk, out_0, out
                     in_=v_tiles[r][:, i, :].rearrange("p (j c) -> p c j", c=XYZ),
                     func=ACT.Square,
                 )
+                nc.gpsimd.tensor_tensor(out=sq[:, 0, :], in0=sq[:, 0, :], in1=sq[:, 1, :], op=ALU.add)
                 sq_tiles[r].append(sq)
 
         def transpose_round(r):
@@ -91,7 +92,7 @@ def tile_multiattentivegvplayer_pa_t_kernel(tc, s, v, Wq, bq, Wk, bk, out_0, out
             for i in range(ROUND):
                 sumsq = psum.tile([P, PACK, P], F32, name="sumsq", bufs=3)
                 for t in range(PACK):
-                    for c in range(XYZ):
+                    for c in (0, XYZ - 1):
                         nc.tensor.matmul(
                             out=sumsq[:, t, :],
                             lhsT=sq_tiles[r][i][:, c, t * P : (t + 1) * P],

@@ -22,7 +22,7 @@ PASSES = 2
 TILES = NODES // P
 ROUND = 2
 ROUNDS = TILES // ROUND
-AHEAD = 10
+AHEAD = 6
 NORM_FLOOR = 1e-4
 SQRT_GUARD = 2.0 ** -100
 
@@ -47,7 +47,7 @@ def tile_multiattentivegvplayer_pa_t_kernel(tc, s, v, Wq, bq, Wk, bk, out_0, out
         loads = ctx.enter_context(tc.tile_pool(name="loads", bufs=AHEAD))
         squares = ctx.enter_context(tc.tile_pool(name="squares", bufs=2 * ROUND))
         operands = ctx.enter_context(tc.tile_pool(name="operands", bufs=2))
-        results = ctx.enter_context(tc.tile_pool(name="results", bufs=3))
+        results = ctx.enter_context(tc.tile_pool(name="results", bufs=4))
         psum = ctx.enter_context(tc.psum_pool(name="psum", bufs=1))
 
         s_tiles = {}
@@ -80,7 +80,7 @@ def tile_multiattentivegvplayer_pa_t_kernel(tc, s, v, Wq, bq, Wk, bk, out_0, out
 
         def transpose_round(r):
             s_words = s_tiles[r][:].bitcast(F32)
-            s_t = psum.tile([P, ROUND, 2, P], F32, name="s_t")
+            s_t = psum.tile([P, ROUND, 2, P], F32, name="s_t", bufs=2)
             for i in range(ROUND):
                 for u in range(2):
                     nc.tensor.transpose(
@@ -90,7 +90,7 @@ def tile_multiattentivegvplayer_pa_t_kernel(tc, s, v, Wq, bq, Wk, bk, out_0, out
                     )
             sumsq_tiles[r] = []
             for i in range(ROUND):
-                sumsq = psum.tile([P, PACK, P], F32, name="sumsq", bufs=3)
+                sumsq = psum.tile([P, PACK, P], F32, name="sumsq", bufs=2)
                 for t in range(PACK):
                     for c in (0, XYZ - 1):
                         nc.tensor.matmul(
@@ -172,14 +172,9 @@ def tile_multiattentivegvplayer_pa_t_kernel(tc, s, v, Wq, bq, Wk, bk, out_0, out
         bias_rows = const.tile([P, 2, OUT], BF16, name="bias_rows")
         nc.vector.memset(bias_rows[:], 0.0)
 
-        load_round(0)
-        for m in range(2):
-            nc.sync.dma_start(
-                out=bias_rows[0:1, m, :], in_=biases[m].rearrange("(o n) -> o n", o=1)
-            )
-        load_round(1)
         w_raw = const.tile([P, 2, PASSES, PACK, OUT], BF16, name="w_raw")
-        for m in range(2):
+
+        def load_weight(m):
             nc.sync.dma_start(
                 out=w_raw[:, m, 0].rearrange("p (u e) n -> p u e n", e=2),
                 in_=weights[m][0:NS, :].rearrange("(u p e) n -> p u e n", u=2, e=2),
@@ -188,7 +183,16 @@ def tile_multiattentivegvplayer_pa_t_kernel(tc, s, v, Wq, bq, Wk, bk, out_0, out
                 out=w_raw[:, m, 1],
                 in_=weights[m][NS : NS + NV, :].rearrange("(t p) n -> p t n", p=P),
             )
-        for r in range(2, AHEAD):
+
+        load_round(0)
+        for m in range(2):
+            nc.sync.dma_start(
+                out=bias_rows[0:1, m, :], in_=biases[m].rearrange("(o n) -> o n", o=1)
+            )
+        for m in range(2):
+            load_round(1 + m)
+            load_weight(m)
+        for r in range(3, AHEAD):
             load_round(r)
 
         bias = const.tile([P, 2, OUT], F32, name="bias")
@@ -200,12 +204,14 @@ def tile_multiattentivegvplayer_pa_t_kernel(tc, s, v, Wq, bq, Wk, bk, out_0, out
         w_grouped = const.tile([P, 2, PASSES, OUT, PACK], BF16, name="w_grouped", align_bytes=64)
         w_codes = const.tile([P, 2, PASSES, OUT], U32, name="w_codes", align_bytes=64)
         w_scales = const.tile([P, 2, PASSES, OUT], U8, name="w_scales", align_bytes=64)
-        for m in range(2):
+
+        def regroup_weight(m):
             for c in range(PASSES):
                 nc.vector.tensor_copy(
                     out=w_grouped[:, m, c], in_=w_raw[:, m, c].rearrange("p t n -> p n t")
                 )
-        for m in range(2):
+
+        def quantise_weight(m):
             nc.vector.quantize_mx(
                 out=w_codes[:, m].rearrange("p c n -> p (c n)").bitcast(FP8X4),
                 scales=w_scales[:, m].rearrange("p c n -> p (c n)"),
@@ -222,8 +228,12 @@ def tile_multiattentivegvplayer_pa_t_kernel(tc, s, v, Wq, bq, Wk, bk, out_0, out
                 floor_round(r - 1)
             if r < ROUNDS:
                 copy_s_round(r, s_t)
+            if r < 2:
+                regroup_weight(r)
             if 1 <= r <= ROUNDS:
                 quantise_round(r - 1)
+            if r < 2:
+                quantise_weight(r)
             if r + 1 < ROUNDS:
                 square_round(r + 1)
             if r >= 2:

@@ -22,6 +22,7 @@ PASSES = 2
 TILES = NODES // P
 ROUND = 2
 ROUNDS = TILES // ROUND
+FIRST_SUMS = 4
 AHEAD = 6
 NORM_FLOOR = 1e-4
 SQRT_GUARD = 2.0 ** -100
@@ -53,6 +54,7 @@ def tile_multiattentivegvplayer_pa_t_kernel(tc, s, v, Wq, bq, Wk, bk, out_0, out
         s_tiles = {}
         v_tiles = {}
         sq_tiles = {}
+        sum_tiles = {}
         sumsq_tiles = {}
         grouped_tiles = {}
         code_tiles = {}
@@ -75,8 +77,15 @@ def tile_multiattentivegvplayer_pa_t_kernel(tc, s, v, Wq, bq, Wk, bk, out_0, out
                     in_=v_tiles[r][:, i, :].rearrange("p (j c) -> p c j", c=XYZ),
                     func=ACT.Square,
                 )
-                nc.gpsimd.tensor_tensor(out=sq[:, 0, :], in0=sq[:, 0, :], in1=sq[:, 1, :], op=ALU.add)
                 sq_tiles[r].append(sq)
+
+        def add_round(r):
+            for i in range(ROUND):
+                sums = grouped_tiles[r - 2][:, i].bitcast(F32).rearrange("p i n u -> p (i n u)")
+                nc.gpsimd.tensor_tensor(
+                    out=sums, in0=sq_tiles[r][i][:, 0, :], in1=sq_tiles[r][i][:, 1, :], op=ALU.add
+                )
+                sum_tiles[r, i] = sums
 
         def transpose_round(r):
             s_words = s_tiles[r][:].bitcast(F32)
@@ -91,21 +100,26 @@ def tile_multiattentivegvplayer_pa_t_kernel(tc, s, v, Wq, bq, Wk, bk, out_0, out
             sumsq_tiles[r] = []
             for i in range(ROUND):
                 sumsq = psum.tile([P, PACK, P], F32, name="sumsq", bufs=2)
+                sq = sq_tiles[r][i]
+                if r < FIRST_SUMS:
+                    planes = [sq[:, c, :] for c in range(XYZ)]
+                else:
+                    planes = [sum_tiles[r, i], sq[:, XYZ - 1, :]]
                 for t in range(PACK):
-                    for c in (0, XYZ - 1):
+                    for c, plane in enumerate(planes):
                         nc.tensor.matmul(
                             out=sumsq[:, t, :],
-                            lhsT=sq_tiles[r][i][:, c, t * P : (t + 1) * P],
+                            lhsT=plane[:, t * P : (t + 1) * P],
                             rhs=ident[:],
                             is_transpose=True,
                             start=(c == 0),
-                            stop=(c == XYZ - 1),
+                            stop=(c == len(planes) - 1),
                         )
                 sumsq_tiles[r].append(sumsq)
             return s_t
 
         def copy_s_round(r, s_t):
-            grouped = operands.tile([P, PASSES, ROUND, P, PACK], BF16, name="grouped", align_bytes=64)
+            grouped = operands.tile([P, PASSES, ROUND, P, PACK], BF16, name="grouped", bufs=4, align_bytes=64)
             nc.vector.tensor_copy(
                 out=grouped[:, 0].bitcast(F32),
                 in_=s_t[:].rearrange("p i u n -> p i n u"),
@@ -226,16 +240,16 @@ def tile_multiattentivegvplayer_pa_t_kernel(tc, s, v, Wq, bq, Wk, bk, out_0, out
                 load_round(r + AHEAD)
             if 1 <= r <= ROUNDS:
                 floor_round(r - 1)
+                quantise_round(r - 1)
             if r < ROUNDS:
                 copy_s_round(r, s_t)
             if r < 2:
                 regroup_weight(r)
-            if 1 <= r <= ROUNDS:
-                quantise_round(r - 1)
-            if r < 2:
                 quantise_weight(r)
             if r + 1 < ROUNDS:
                 square_round(r + 1)
+                if r + 1 >= FIRST_SUMS:
+                    add_round(r + 1)
             if r >= 2:
                 project_round(r - 2)
             if r < ROUNDS:

@@ -23,7 +23,10 @@ TILES = NODES // P
 ROUND = 2
 ROUNDS = TILES // ROUND
 FIRST_SUMS = 4
-AHEAD = 6
+FIRST_LOADS = 4
+GROUP = 2
+GROUPS = (ROUNDS - FIRST_LOADS) // GROUP
+GROUPS_HELD = 4
 NORM_FLOOR = 1e-4
 SQRT_GUARD = 2.0 ** -100
 
@@ -45,7 +48,8 @@ def tile_multiattentivegvplayer_pa_t_kernel(tc, s, v, Wq, bq, Wk, bk, out_0, out
     with ExitStack() as ctx:
         ctx.enter_context(tc.manual_schedule())
         const = ctx.enter_context(tc.tile_pool(name="const", bufs=1))
-        loads = ctx.enter_context(tc.tile_pool(name="loads", bufs=AHEAD))
+        first_loads = ctx.enter_context(tc.tile_pool(name="first_loads", bufs=FIRST_LOADS))
+        group_loads = ctx.enter_context(tc.tile_pool(name="group_loads", bufs=GROUPS_HELD))
         squares = ctx.enter_context(tc.tile_pool(name="squares", bufs=2 * ROUND))
         operands = ctx.enter_context(tc.tile_pool(name="operands", bufs=2))
         results = ctx.enter_context(tc.tile_pool(name="results", bufs=4))
@@ -59,14 +63,22 @@ def tile_multiattentivegvplayer_pa_t_kernel(tc, s, v, Wq, bq, Wk, bk, out_0, out
         grouped_tiles = {}
         code_tiles = {}
 
+        def load_rounds(pool, r, rounds):
+            n = rounds * ROUND
+            node_tiles = slice(r * ROUND, r * ROUND + n)
+            v_sb = pool.tile([P, n, NV * XYZ], BF16, name="v_sb")
+            nc.sync.dma_start(out=v_sb[:], in_=v_view[:, node_tiles, :])
+            s_sb = pool.tile([P, n, NS], BF16, name="s_sb")
+            nc.sync.dma_start(out=s_sb[:], in_=s_view[:, node_tiles, :])
+            for j in range(rounds):
+                v_tiles[r + j] = v_sb[:, j * ROUND : (j + 1) * ROUND, :]
+                s_tiles[r + j] = s_sb[:, j * ROUND : (j + 1) * ROUND, :]
+
         def load_round(r):
-            tiles_of_round = slice(r * ROUND, (r + 1) * ROUND)
-            v_sb = loads.tile([P, ROUND, NV * XYZ], BF16, name="v_sb")
-            nc.sync.dma_start(out=v_sb[:], in_=v_view[:, tiles_of_round, :])
-            s_sb = loads.tile([P, ROUND, NS], BF16, name="s_sb")
-            nc.sync.dma_start(out=s_sb[:], in_=s_view[:, tiles_of_round, :])
-            v_tiles[r] = v_sb
-            s_tiles[r] = s_sb
+            load_rounds(first_loads, r, 1)
+
+        def load_group(g):
+            load_rounds(group_loads, FIRST_LOADS + g * GROUP, GROUP)
 
         def square_round(r):
             sq_tiles[r] = []
@@ -88,7 +100,7 @@ def tile_multiattentivegvplayer_pa_t_kernel(tc, s, v, Wq, bq, Wk, bk, out_0, out
                 sum_tiles[r, i] = sums
 
         def transpose_round(r):
-            s_words = s_tiles[r][:].bitcast(F32)
+            s_words = s_tiles[r].bitcast(F32)
             s_t = psum.tile([P, ROUND, 2, P], F32, name="s_t", bufs=2)
             for i in range(ROUND):
                 for u in range(2):
@@ -206,8 +218,10 @@ def tile_multiattentivegvplayer_pa_t_kernel(tc, s, v, Wq, bq, Wk, bk, out_0, out
         for m in range(2):
             load_round(1 + m)
             load_weight(m)
-        for r in range(3, AHEAD):
+        for r in range(3, FIRST_LOADS):
             load_round(r)
+        for g in range(GROUPS_HELD):
+            load_group(g)
 
         bias = const.tile([P, 2, OUT], F32, name="bias")
         for m in range(2):
@@ -236,8 +250,9 @@ def tile_multiattentivegvplayer_pa_t_kernel(tc, s, v, Wq, bq, Wk, bk, out_0, out
         for r in range(ROUNDS + 2):
             if r < ROUNDS:
                 s_t = transpose_round(r)
-            if r + AHEAD < ROUNDS:
-                load_round(r + AHEAD)
+            groups_read, rest = divmod(r + 1 - FIRST_LOADS, GROUP)
+            if groups_read >= 1 and rest == 0 and groups_read - 1 + GROUPS_HELD < GROUPS:
+                load_group(groups_read - 1 + GROUPS_HELD)
             if 1 <= r <= ROUNDS:
                 floor_round(r - 1)
                 quantise_round(r - 1)

@@ -22,7 +22,7 @@ PASSES = 2
 TILES = NODES // P
 ROUND = 2
 ROUNDS = TILES // ROUND
-FIRST_SUMS = 4
+FIRST_SUMS = 3
 FIRST_LOADS = 4
 GROUP = 2
 GROUPS = (ROUNDS - FIRST_LOADS) // GROUP
@@ -48,7 +48,7 @@ def tile_multiattentivegvplayer_pa_t_kernel(tc, s, v, Wq, bq, Wk, bk, out_0, out
     with ExitStack() as ctx:
         ctx.enter_context(tc.manual_schedule())
         const = ctx.enter_context(tc.tile_pool(name="const", bufs=1))
-        first_loads = ctx.enter_context(tc.tile_pool(name="first_loads", bufs=FIRST_LOADS))
+        first_loads = ctx.enter_context(tc.tile_pool(name="first_loads", bufs=1))
         group_loads = ctx.enter_context(tc.tile_pool(name="group_loads", bufs=GROUPS_HELD))
         squares = ctx.enter_context(tc.tile_pool(name="squares", bufs=2 * ROUND))
         operands = ctx.enter_context(tc.tile_pool(name="operands", bufs=2))
@@ -63,56 +63,57 @@ def tile_multiattentivegvplayer_pa_t_kernel(tc, s, v, Wq, bq, Wk, bk, out_0, out
         grouped_tiles = {}
         code_tiles = {}
 
-        def load_rounds(pool, r, rounds):
-            n = rounds * ROUND
-            node_tiles = slice(r * ROUND, r * ROUND + n)
-            v_sb = pool.tile([P, n, NV * XYZ], BF16, name="v_sb")
-            nc.sync.dma_start(out=v_sb[:], in_=v_view[:, node_tiles, :])
-            s_sb = pool.tile([P, n, NS], BF16, name="s_sb")
-            nc.sync.dma_start(out=s_sb[:], in_=s_view[:, node_tiles, :])
-            for j in range(rounds):
-                v_tiles[r + j] = v_sb[:, j * ROUND : (j + 1) * ROUND, :]
-                s_tiles[r + j] = s_sb[:, j * ROUND : (j + 1) * ROUND, :]
+        def load_v_tile(t):
+            v_sb = first_loads.tile([P, NV * XYZ], BF16, name="v_first", bufs=FIRST_LOADS * ROUND)
+            nc.sync.dma_start(out=v_sb[:], in_=v_view[:, t, :])
+            v_tiles[t] = v_sb[:]
 
-        def load_round(r):
-            load_rounds(first_loads, r, 1)
+        def load_s_round(r):
+            s_sb = first_loads.tile([P, ROUND, NS], BF16, name="s_first", bufs=FIRST_LOADS)
+            nc.sync.dma_start(out=s_sb[:], in_=s_view[:, r * ROUND : (r + 1) * ROUND, :])
+            for i in range(ROUND):
+                s_tiles[r * ROUND + i] = s_sb[:, i, :]
 
         def load_group(g):
-            load_rounds(group_loads, FIRST_LOADS + g * GROUP, GROUP)
+            n = GROUP * ROUND
+            t0 = FIRST_LOADS * ROUND + g * n
+            v_sb = group_loads.tile([P, n, NV * XYZ], BF16, name="v_sb")
+            nc.sync.dma_start(out=v_sb[:], in_=v_view[:, t0 : t0 + n, :])
+            s_sb = group_loads.tile([P, n, NS], BF16, name="s_sb")
+            nc.sync.dma_start(out=s_sb[:], in_=s_view[:, t0 : t0 + n, :])
+            for j in range(n):
+                v_tiles[t0 + j] = v_sb[:, j, :]
+                s_tiles[t0 + j] = s_sb[:, j, :]
 
-        def square_round(r):
-            sq_tiles[r] = []
-            for i in range(ROUND):
-                sq = squares.tile([P, XYZ, NV], F32, name="sq")
-                nc.scalar.activation(
-                    out=sq[:],
-                    in_=v_tiles[r][:, i, :].rearrange("p (j c) -> p c j", c=XYZ),
-                    func=ACT.Square,
-                )
-                sq_tiles[r].append(sq)
+        def square_tile(r, i):
+            sq = squares.tile([P, XYZ, NV], F32, name="sq")
+            nc.scalar.activation(
+                out=sq[:],
+                in_=v_tiles[r * ROUND + i].rearrange("p (j c) -> p c j", c=XYZ),
+                func=ACT.Square,
+            )
+            sq_tiles[r, i] = sq
 
-        def add_round(r):
-            for i in range(ROUND):
-                sums = grouped_tiles[r - 2][:, i].bitcast(F32).rearrange("p i n u -> p (i n u)")
-                nc.gpsimd.tensor_tensor(
-                    out=sums, in0=sq_tiles[r][i][:, 0, :], in1=sq_tiles[r][i][:, 1, :], op=ALU.add
-                )
-                sum_tiles[r, i] = sums
+        def add_tile(r, i):
+            sq = sq_tiles[r, i]
+            sums = grouped_tiles[r - 2][:, i].bitcast(F32).rearrange("p i n u -> p (i n u)")
+            nc.gpsimd.tensor_tensor(out=sums, in0=sq[:, 0, :], in1=sq[:, 1, :], op=ALU.add)
+            sum_tiles[r, i] = sums
 
         def transpose_round(r):
-            s_words = s_tiles[r].bitcast(F32)
             s_t = psum.tile([P, ROUND, 2, P], F32, name="s_t", bufs=2)
             for i in range(ROUND):
+                s_words = s_tiles[r * ROUND + i].bitcast(F32)
                 for u in range(2):
                     nc.tensor.transpose(
                         out=s_t[:, i, u, :],
-                        in_=s_words[:, i, u * P : (u + 1) * P],
+                        in_=s_words[:, u * P : (u + 1) * P],
                         identity=ident[:],
                     )
             sumsq_tiles[r] = []
             for i in range(ROUND):
                 sumsq = psum.tile([P, PACK, P], F32, name="sumsq", bufs=2)
-                sq = sq_tiles[r][i]
+                sq = sq_tiles[r, i]
                 if r < FIRST_SUMS:
                     planes = [sq[:, c, :] for c in range(XYZ)]
                 else:
@@ -131,29 +132,28 @@ def tile_multiattentivegvplayer_pa_t_kernel(tc, s, v, Wq, bq, Wk, bk, out_0, out
             return s_t
 
         def copy_s_round(r, s_t):
-            grouped = operands.tile([P, PASSES, ROUND, P, PACK], BF16, name="grouped", bufs=4, align_bytes=64)
+            grouped = operands.tile([P, PASSES, ROUND, P, PACK], BF16, name="grouped", bufs=4, align_bytes=256)
             nc.vector.tensor_copy(
                 out=grouped[:, 0].bitcast(F32),
                 in_=s_t[:].rearrange("p i u n -> p i n u"),
             )
             grouped_tiles[r] = grouped
 
-        def root_round(r):
-            for i in range(ROUND):
-                nc.scalar.activation(
-                    out=grouped_tiles[r][:, 1, i],
-                    in_=sumsq_tiles[r][i][:].rearrange("p t n -> p n t"),
-                    func=ACT.Sqrt,
-                    bias=guard[:],
-                )
+        def root_tile(r, i):
+            nc.scalar.activation(
+                out=grouped_tiles[r][:, 1, i],
+                in_=sumsq_tiles[r][i][:].rearrange("p t n -> p n t"),
+                func=ACT.Sqrt,
+                bias=guard[:],
+            )
 
         def floor_round(r):
             norms = grouped_tiles[r][:, 1]
             nc.vector.tensor_scalar_max(out=norms, in0=norms, scalar1=NORM_FLOOR)
 
         def quantise_round(r):
-            codes = operands.tile([P, PASSES, ROUND, P], U32, name="codes", bufs=3, align_bytes=64)
-            scales = operands.tile([P, PASSES, ROUND, P], U8, name="scales", bufs=3, align_bytes=64)
+            codes = operands.tile([P, PASSES, ROUND, P], U32, name="codes", bufs=3, align_bytes=256)
+            scales = operands.tile([P, PASSES, ROUND, P], U8, name="scales", bufs=3, align_bytes=256)
             nc.vector.quantize_mx(
                 out=codes[:].rearrange("p c i n -> p (c i n)").bitcast(FP8X4),
                 scales=scales[:].rearrange("p c i n -> p (c i n)"),
@@ -184,8 +184,13 @@ def tile_multiattentivegvplayer_pa_t_kernel(tc, s, v, Wq, bq, Wk, bk, out_0, out
                     nc.vector.tensor_tensor(
                         out=out_sb[m][:, i, :], in0=acc[:], in1=bias[:, m, :], op=ALU.add
                     )
-            for m in range(2):
-                nc.sync.dma_start(out=out_views[m][:, tiles_of_round, :], in_=out_sb[m][:])
+                    if r == ROUNDS - 1:
+                        nc.sync.dma_start(
+                            out=out_views[m][:, r * ROUND + i, :], in_=out_sb[m][:, i, :]
+                        )
+            if r < ROUNDS - 1:
+                for m in range(2):
+                    nc.sync.dma_start(out=out_views[m][:, tiles_of_round, :], in_=out_sb[m][:])
 
         guard = const.tile([P, 1], F32, name="guard")
         nc.vector.memset(guard[:], SQRT_GUARD)
@@ -200,44 +205,50 @@ def tile_multiattentivegvplayer_pa_t_kernel(tc, s, v, Wq, bq, Wk, bk, out_0, out
 
         w_raw = const.tile([P, 2, PASSES, PACK, OUT], BF16, name="w_raw")
 
-        def load_weight(m):
-            nc.sync.dma_start(
-                out=w_raw[:, m, 0].rearrange("p (u e) n -> p u e n", e=2),
-                in_=weights[m][0:NS, :].rearrange("(u p e) n -> p u e n", u=2, e=2),
-            )
-            nc.sync.dma_start(
-                out=w_raw[:, m, 1],
-                in_=weights[m][NS : NS + NV, :].rearrange("(t p) n -> p t n", p=P),
-            )
+        def load_weight_pass(m, c):
+            if c == 0:
+                nc.sync.dma_start(
+                    out=w_raw[:, m, 0].rearrange("p (u e) n -> p u e n", e=2),
+                    in_=weights[m][0:NS, :].rearrange("(u p e) n -> p u e n", u=2, e=2),
+                )
+            else:
+                nc.sync.dma_start(
+                    out=w_raw[:, m, 1],
+                    in_=weights[m][NS : NS + NV, :].rearrange("(t p) n -> p t n", p=P),
+                )
 
-        load_round(0)
-        for m in range(2):
-            nc.sync.dma_start(
-                out=bias_rows[0:1, m, :], in_=biases[m].rearrange("(o n) -> o n", o=1)
-            )
-        for m in range(2):
-            load_round(1 + m)
-            load_weight(m)
-        for r in range(3, FIRST_LOADS):
-            load_round(r)
+        for r in range(FIRST_LOADS):
+            for i in range(ROUND):
+                if 1 <= r <= 2:
+                    load_weight_pass(r - 1, i)
+                load_v_tile(r * ROUND + i)
+            if r == 2:
+                for m in range(2):
+                    nc.sync.dma_start(
+                        out=bias_rows[0:1, m, :], in_=biases[m].rearrange("(o n) -> o n", o=1)
+                    )
+            load_s_round(r)
         for g in range(GROUPS_HELD):
             load_group(g)
 
         bias = const.tile([P, 2, OUT], F32, name="bias")
-        for m in range(2):
-            acc = psum.tile([P, OUT], F32, name="acc", bufs=4)
-            nc.tensor.matmul(out=acc[:], lhsT=ones[:], rhs=bias_rows[:, m, :], start=True, stop=True)
-            nc.vector.tensor_copy(out=bias[:, m, :], in_=acc[:])
 
-        w_grouped = const.tile([P, 2, PASSES, OUT, PACK], BF16, name="w_grouped", align_bytes=64)
-        w_codes = const.tile([P, 2, PASSES, OUT], U32, name="w_codes", align_bytes=64)
-        w_scales = const.tile([P, 2, PASSES, OUT], U8, name="w_scales", align_bytes=64)
-
-        def regroup_weight(m):
-            for c in range(PASSES):
-                nc.vector.tensor_copy(
-                    out=w_grouped[:, m, c], in_=w_raw[:, m, c].rearrange("p t n -> p n t")
+        def spread_biases():
+            for m in range(2):
+                acc = psum.tile([P, OUT], F32, name="acc", bufs=4)
+                nc.tensor.matmul(
+                    out=acc[:], lhsT=ones[:], rhs=bias_rows[:, m, :], start=True, stop=True
                 )
+                nc.vector.tensor_copy(out=bias[:, m, :], in_=acc[:])
+
+        w_grouped = const.tile([P, 2, PASSES, OUT, PACK], BF16, name="w_grouped", align_bytes=256)
+        w_codes = const.tile([P, 2, PASSES, OUT], U32, name="w_codes", align_bytes=256)
+        w_scales = const.tile([P, 2, PASSES, OUT], U8, name="w_scales", align_bytes=256)
+
+        def regroup_weight_pass(m, c):
+            nc.vector.tensor_copy(
+                out=w_grouped[:, m, c], in_=w_raw[:, m, c].rearrange("p t n -> p n t")
+            )
 
         def quantise_weight(m):
             nc.vector.quantize_mx(
@@ -246,26 +257,32 @@ def tile_multiattentivegvplayer_pa_t_kernel(tc, s, v, Wq, bq, Wk, bk, out_0, out
                 in_=w_grouped[:, m].rearrange("p c n t -> p (c n t)"),
             )
 
-        square_round(0)
+        for i in range(ROUND):
+            square_tile(0, i)
         for r in range(ROUNDS + 2):
+            if r == 2:
+                spread_biases()
             if r < ROUNDS:
                 s_t = transpose_round(r)
             groups_read, rest = divmod(r + 1 - FIRST_LOADS, GROUP)
             if groups_read >= 1 and rest == 0 and groups_read - 1 + GROUPS_HELD < GROUPS:
                 load_group(groups_read - 1 + GROUPS_HELD)
+            if r < 2:
+                regroup_weight_pass(r, 0)
             if 1 <= r <= ROUNDS:
                 floor_round(r - 1)
                 quantise_round(r - 1)
             if r < ROUNDS:
                 copy_s_round(r, s_t)
             if r < 2:
-                regroup_weight(r)
+                regroup_weight_pass(r, 1)
                 quantise_weight(r)
-            if r + 1 < ROUNDS:
-                square_round(r + 1)
-                if r + 1 >= FIRST_SUMS:
-                    add_round(r + 1)
+            for i in range(ROUND):
+                if r + 1 < ROUNDS:
+                    square_tile(r + 1, i)
+                    if r + 1 >= FIRST_SUMS:
+                        add_tile(r + 1, i)
+                if r < ROUNDS:
+                    root_tile(r, i)
             if r >= 2:
                 project_round(r - 2)
-            if r < ROUNDS:
-                root_round(r)

from contextlib import ExitStack

import concourse.mybir as mybir
from concourse.masks import make_identity

F32 = mybir.dt.float32
BF16 = mybir.dt.bfloat16
U32 = mybir.dt.uint32
U8 = mybir.dt.uint8
FP8X4 = mybir.dt.float8_e4m3fn_x4
ACT = mybir.ActivationFunctionType
ALU = mybir.AluOpType

P = 128
PACK = 4
NODES = 4096
NS = 512
NV = 512
XYZ = 3
OUT = 512
PASSES = 2
TILES = NODES // P
ROUND = 2
ROUNDS = TILES // ROUND
FIRST_SUMS = 3
FIRST_LOADS = 4
GROUP = 2
GROUPS = (ROUNDS - FIRST_LOADS) // GROUP
GROUPS_HELD = 4
NORM_FLOOR = 1e-4
SQRT_GUARD = 2.0 ** -100

FLOPS = 2 * NODES * (NS + NV) * (2 * OUT)


def tile_multiattentivegvplayer_pa_t_kernel(tc, s, v, Wq, bq, Wk, bk, out_0, out_1):
    nc = tc.nc
    weights = (Wq, Wk)
    biases = (bq, bk)

    s_view = s.rearrange("(p t) k -> p t k", t=TILES)
    v_view = v.rearrange("(p t) j c -> p t (j c)", t=TILES)
    out_views = (
        out_0.rearrange("(p t) h d -> p t (h d)", t=TILES),
        out_1.rearrange("(p t) h d -> p t (h d)", t=TILES),
    )

    with ExitStack() as ctx:
        ctx.enter_context(tc.manual_schedule())
        const = ctx.enter_context(tc.tile_pool(name="const", bufs=1))
        first_loads = ctx.enter_context(tc.tile_pool(name="first_loads", bufs=1))
        group_loads = ctx.enter_context(tc.tile_pool(name="group_loads", bufs=GROUPS_HELD))
        squares = ctx.enter_context(tc.tile_pool(name="squares", bufs=2 * ROUND))
        operands = ctx.enter_context(tc.tile_pool(name="operands", bufs=2))
        results = ctx.enter_context(tc.tile_pool(name="results", bufs=4))
        psum = ctx.enter_context(tc.psum_pool(name="psum", bufs=1))

        s_tiles = {}
        v_tiles = {}
        sq_tiles = {}
        sum_tiles = {}
        sumsq_tiles = {}
        grouped_tiles = {}
        code_tiles = {}

        def load_v_tile(t):
            v_sb = first_loads.tile([P, NV * XYZ], BF16, name="v_first", bufs=FIRST_LOADS * ROUND)
            nc.sync.dma_start(out=v_sb[:], in_=v_view[:, t, :])
            v_tiles[t] = v_sb[:]

        def load_s_round(r):
            s_sb = first_loads.tile([P, ROUND, NS], BF16, name="s_first", bufs=FIRST_LOADS)
            nc.sync.dma_start(out=s_sb[:], in_=s_view[:, r * ROUND : (r + 1) * ROUND, :])
            for i in range(ROUND):
                s_tiles[r * ROUND + i] = s_sb[:, i, :]

        def load_group(g):
            n = GROUP * ROUND
            t0 = FIRST_LOADS * ROUND + g * n
            v_sb = group_loads.tile([P, n, NV * XYZ], BF16, name="v_sb")
            nc.sync.dma_start(out=v_sb[:], in_=v_view[:, t0 : t0 + n, :])
            s_sb = group_loads.tile([P, n, NS], BF16, name="s_sb")
            nc.sync.dma_start(out=s_sb[:], in_=s_view[:, t0 : t0 + n, :])
            for j in range(n):
                v_tiles[t0 + j] = v_sb[:, j, :]
                s_tiles[t0 + j] = s_sb[:, j, :]

        def square_tile(r, i):
            sq = squares.tile([P, XYZ, NV], F32, name="sq")
            nc.scalar.activation(
                out=sq[:],
                in_=v_tiles[r * ROUND + i].rearrange("p (j c) -> p c j", c=XYZ),
                func=ACT.Square,
            )
            sq_tiles[r, i] = sq

        def add_tile(r, i):
            sq = sq_tiles[r, i]
            sums = grouped_tiles[r - 2][:, i].bitcast(F32).rearrange("p i n u -> p (i n u)")
            nc.gpsimd.tensor_tensor(out=sums, in0=sq[:, 0, :], in1=sq[:, 1, :], op=ALU.add)
            sum_tiles[r, i] = sums

        def transpose_round(r):
            s_t = psum.tile([P, ROUND, 2, P], F32, name="s_t", bufs=2)
            for i in range(ROUND):
                s_words = s_tiles[r * ROUND + i].bitcast(F32)
                for u in range(2):
                    nc.tensor.transpose(
                        out=s_t[:, i, u, :],
                        in_=s_words[:, u * P : (u + 1) * P],
                        identity=ident[:],
                    )
            sumsq_tiles[r] = []
            for i in range(ROUND):
                sumsq = psum.tile([P, PACK, P], F32, name="sumsq", bufs=2)
                sq = sq_tiles[r, i]
                if r < FIRST_SUMS:
                    planes = [sq[:, c, :] for c in range(XYZ)]
                else:
                    planes = [sum_tiles[r, i], sq[:, XYZ - 1, :]]
                for t in range(PACK):
                    for c, plane in enumerate(planes):
                        nc.tensor.matmul(
                            out=sumsq[:, t, :],
                            lhsT=plane[:, t * P : (t + 1) * P],
                            rhs=ident[:],
                            is_transpose=True,
                            start=(c == 0),
                            stop=(c == len(planes) - 1),
                        )
                sumsq_tiles[r].append(sumsq)
            return s_t

        def copy_s_round(r, s_t):
            grouped = operands.tile([P, PASSES, ROUND, P, PACK], BF16, name="grouped", bufs=4, align_bytes=256)
            nc.vector.tensor_copy(
                out=grouped[:, 0].bitcast(F32),
                in_=s_t[:].rearrange("p i u n -> p i n u"),
            )
            grouped_tiles[r] = grouped

        def root_tile(r, i):
            nc.scalar.activation(
                out=grouped_tiles[r][:, 1, i],
                in_=sumsq_tiles[r][i][:].rearrange("p t n -> p n t"),
                func=ACT.Sqrt,
                bias=guard[:],
            )

        def floor_round(r):
            norms = grouped_tiles[r][:, 1]
            nc.vector.tensor_scalar_max(out=norms, in0=norms, scalar1=NORM_FLOOR)

        def quantise_round(r):
            codes = operands.tile([P, PASSES, ROUND, P], U32, name="codes", bufs=3, align_bytes=256)
            scales = operands.tile([P, PASSES, ROUND, P], U8, name="scales", bufs=3, align_bytes=256)
            nc.vector.quantize_mx(
                out=codes[:].rearrange("p c i n -> p (c i n)").bitcast(FP8X4),
                scales=scales[:].rearrange("p c i n -> p (c i n)"),
                in_=grouped_tiles[r][:].rearrange("p c i n t -> p (c i n t)"),
            )
            code_tiles[r] = (codes, scales)

        def project_round(r):
            codes, scales = code_tiles[r]
            tiles_of_round = slice(r * ROUND, (r + 1) * ROUND)
            out_sb = [
                results.tile([P, ROUND, OUT], F32, name="q_sb"),
                results.tile([P, ROUND, OUT], F32, name="k_sb"),
            ]
            for i in range(ROUND):
                for m in range(2):
                    acc = psum.tile([P, OUT], F32, name="acc", bufs=4)
                    for c in range(PASSES):
                        nc.tensor.matmul_mx(
                            out=acc[:],
                            lhsT=codes[:, c, i, :].bitcast(FP8X4),
                            lhsT_scale=scales[:, c, i, :],
                            rhs=w_codes[:, m, c, :].bitcast(FP8X4),
                            rhs_scale=w_scales[:, m, c, :],
                            start=(c == 0),
                            stop=(c == PASSES - 1),
                        )
                    nc.vector.tensor_tensor(
                        out=out_sb[m][:, i, :], in0=acc[:], in1=bias[:, m, :], op=ALU.add
                    )
                    if r == ROUNDS - 1:
                        nc.sync.dma_start(
                            out=out_views[m][:, r * ROUND + i, :], in_=out_sb[m][:, i, :]
                        )
            if r < ROUNDS - 1:
                for m in range(2):
                    nc.sync.dma_start(out=out_views[m][:, tiles_of_round, :], in_=out_sb[m][:])

        guard = const.tile([P, 1], F32, name="guard")
        nc.vector.memset(guard[:], SQRT_GUARD)
        warm = const.tile([P, 1], F32, name="warm")
        nc.scalar.activation(out=warm[:], in_=guard[:], func=ACT.Sqrt)
        ident = const.tile([P, P], F32, name="ident")
        make_identity(nc, ident[:])
        ones = const.tile([P, P], BF16, name="ones")
        nc.vector.memset(ones[:], 1.0)
        bias_rows = const.tile([P, 2, OUT], BF16, name="bias_rows")
        nc.vector.memset(bias_rows[:], 0.0)

        w_raw = const.tile([P, 2, PASSES, PACK, OUT], BF16, name="w_raw")

        def load_weight_pass(m, c):
            if c == 0:
                nc.sync.dma_start(
                    out=w_raw[:, m, 0].rearrange("p (u e) n -> p u e n", e=2),
                    in_=weights[m][0:NS, :].rearrange("(u p e) n -> p u e n", u=2, e=2),
                )
            else:
                nc.sync.dma_start(
                    out=w_raw[:, m, 1],
                    in_=weights[m][NS : NS + NV, :].rearrange("(t p) n -> p t n", p=P),
                )

        for r in range(FIRST_LOADS):
            for i in range(ROUND):
                if 1 <= r <= 2:
                    load_weight_pass(r - 1, i)
                load_v_tile(r * ROUND + i)
            if r == 2:
                for m in range(2):
                    nc.sync.dma_start(
                        out=bias_rows[0:1, m, :], in_=biases[m].rearrange("(o n) -> o n", o=1)
                    )
            load_s_round(r)
        for g in range(GROUPS_HELD):
            load_group(g)

        bias = const.tile([P, 2, OUT], F32, name="bias")

        def spread_biases():
            for m in range(2):
                acc = psum.tile([P, OUT], F32, name="acc", bufs=4)
                nc.tensor.matmul(
                    out=acc[:], lhsT=ones[:], rhs=bias_rows[:, m, :], start=True, stop=True
                )
                nc.vector.tensor_copy(out=bias[:, m, :], in_=acc[:])

        w_grouped = const.tile([P, 2, PASSES, OUT, PACK], BF16, name="w_grouped", align_bytes=256)
        w_codes = const.tile([P, 2, PASSES, OUT], U32, name="w_codes", align_bytes=256)
        w_scales = const.tile([P, 2, PASSES, OUT], U8, name="w_scales", align_bytes=256)

        def regroup_weight_pass(m, c):
            nc.vector.tensor_copy(
                out=w_grouped[:, m, c], in_=w_raw[:, m, c].rearrange("p t n -> p n t")
            )

        def quantise_weight(m):
            nc.vector.quantize_mx(
                out=w_codes[:, m].rearrange("p c n -> p (c n)").bitcast(FP8X4),
                scales=w_scales[:, m].rearrange("p c n -> p (c n)"),
                in_=w_grouped[:, m].rearrange("p c n t -> p (c n t)"),
            )

        for i in range(ROUND):
            square_tile(0, i)
        for r in range(ROUNDS + 2):
            if r == 2:
                spread_biases()
            if r < ROUNDS:
                s_t = transpose_round(r)
            groups_read, rest = divmod(r + 1 - FIRST_LOADS, GROUP)
            if groups_read >= 1 and rest == 0 and groups_read - 1 + GROUPS_HELD < GROUPS:
                load_group(groups_read - 1 + GROUPS_HELD)
            if r < 2:
                regroup_weight_pass(r, 0)
            if 1 <= r <= ROUNDS:
                floor_round(r - 1)
                quantise_round(r - 1)
            if r < ROUNDS:
                copy_s_round(r, s_t)
            if r < 2:
                regroup_weight_pass(r, 1)
                quantise_weight(r)
            for i in range(ROUND):
                if r + 1 < ROUNDS:
                    square_tile(r + 1, i)
                    if r + 1 >= FIRST_SUMS:
                        add_tile(r + 1, i)
                if r < ROUNDS:
                    root_tile(r, i)
            if r >= 2:
                project_round(r - 2)
